import numpy as np
import ml_dtypes


def mxq(x, axis, fmt="e4m3"):
    dtype, down = {"e4m3": (ml_dtypes.float8_e4m3fn, 7), "e5m2": (ml_dtypes.float8_e5m2, 14)}[fmt]
    v = np.moveaxis(np.asarray(x, np.float32).astype(ml_dtypes.bfloat16).astype(np.float64), axis, -1)
    blocks = v.reshape(v.shape[:-1] + (-1, 32))
    amax = np.abs(blocks).max(-1, keepdims=True)
    byte = np.maximum(np.where(amax > 0, np.frexp(amax)[1] - 1 + 127, 0) - down, 1)
    scale = np.exp2(byte - 127.0)
    codes = (blocks / scale).astype(np.float32).astype(dtype).astype(np.float64)
    return np.moveaxis((codes * scale).reshape(v.shape), -1, axis)


WIDE = False


def mx_kscale(k):
    if not WIDE:
        return np.ones(k)
    levels = np.array([10, -10, 5, -5, 0])
    a = np.random.permutation(np.resize(levels, k // 512 * 4)).reshape(k // 512, 4)
    idx = np.arange(k)
    return np.exp2(a[idx // 512, idx % 128 // 32])


BF16 = ml_dtypes.bfloat16


def bf(x):
    return np.asarray(x, np.float32).astype(BF16)


def f64(x):
    return np.asarray(x).astype(np.float64)


B, O, A, H, Z = 4096, 512, 512, 512, 128
CLAMP = 10.0
LV_LO, LV_HI = -12.0, 2.0


def setup_inputs():
    s, t = mx_kscale(O + H), mx_kscale(H)
    return {
        "x_t": bf(np.random.standard_normal((B, O)) * s[:O]),
        "h_prev": bf(np.random.standard_normal((B, H)) * s[O:]),
        "eps": bf(np.random.standard_normal((B, Z))),
        "enc_w1": bf(np.random.standard_normal((H, O + H)) / np.sqrt(O + H) * t[:, None] / s[None, :]),
        "enc_b1": bf(np.random.standard_normal(H) * 0.1 * t),
        "enc_w2": bf(np.random.standard_normal((2 * Z, H)) * 1.4 / np.sqrt(H) / t[None, :]),
        "enc_b2": bf(np.concatenate([np.random.standard_normal(Z) * 0.1, np.random.uniform(LV_LO, LV_HI, Z)])),
        "mu_p": bf(np.random.standard_normal((B, Z)) * 0.7),
        "logvar_p": bf(np.random.standard_normal((B, Z)) * 0.7),
    }


def reference(x_t, h_prev, eps, enc_w1, enc_b1, enc_w2, enc_b2, mu_p, logvar_p):
    mu_p, logvar_p = f64(mu_p), f64(logvar_p)
    xh = np.concatenate([f64(x_t), f64(h_prev)], -1)
    hid = np.maximum((mxq(xh, 1, "e4m3") @ mxq(f64(enc_w1), 1, "e4m3").T) + f64(enc_b1), 0.0)
    stats = (mxq(hid, 1, "e4m3") @ mxq(f64(enc_w2), 1, "e4m3").T) + f64(enc_b2)
    mu_q = stats[:, :Z]
    logvar_q = np.clip(stats[:, Z:], -CLAMP, CLAMP)
    std_q = np.exp(0.5 * logvar_q)
    z_t = mu_q + f64(eps) * std_q
    var_p = np.exp(logvar_p)
    kl = 0.5 * np.sum((mu_q - mu_p) ** 2 / var_p + np.exp(logvar_q) / var_p + (logvar_p - logvar_q) - 1.0, axis=-1)
    return z_t, mu_q, logvar_q, kl

@@ -1,0 +1,288 @@
+from contextlib import ExitStack
+
+import concourse.mybir as mybir
+from concourse.masks import make_identity
+
+F32 = mybir.dt.float32
+BF16 = mybir.dt.bfloat16
+U32 = mybir.dt.uint32
+U8 = mybir.dt.uint8
+FP8X4 = mybir.dt.float8_e4m3fn_x4
+ACT = mybir.ActivationFunctionType
+ALU = mybir.AluOpType
+
+P = 128
+B, O, H, Z = 4096, 512, 512, 128
+CLAMP = 10.0
+PACK = 4
+K_PASS = P * PACK
+WORDS = K_PASS // 2
+TILES = B // P
+TPC = 4
+CHUNK = TPC * P
+NCH = TILES // TPC
+HALF_TILES = TILES // 2
+H_TILES = H // P
+
+FLOPS = 2 * B * (O + H) * H + 2 * B * H * 2 * Z
+
+
+def words_onto_partitions(nc, bank, ident, word_blocks, grouped_words, copy):
+    for s in range(2):
+        for u in range(2):
+            nc.tensor.transpose(bank[:, u, s * P : (s + 1) * P], word_blocks[s][u], ident)
+    copy(
+        out=grouped_words.rearrange("p (c u) -> p c u", u=2),
+        in_=bank.rearrange("p u c -> p c u"),
+    )
+
+
+def tile_vrnncell_pa_t_kernel(
+    tc, x_t, h_prev, eps, enc_w1, enc_b1, enc_w2, enc_b2, mu_p, logvar_p, z_out, mu_out, lv_out, kl_out
+):
+    nc = tc.nc
+    with ExitStack() as ctx:
+        const = ctx.enter_context(tc.tile_pool(name="const", bufs=1))
+        resident = ctx.enter_context(tc.tile_pool(name="resident", bufs=NCH))
+        prior = ctx.enter_context(tc.tile_pool(name="prior", bufs=2))
+        xq = ctx.enter_context(tc.tile_pool(name="xq", bufs=2))
+        hq = ctx.enter_context(tc.tile_pool(name="hq", bufs=2))
+        outp = ctx.enter_context(tc.tile_pool(name="outp", bufs=3))
+        scr = ctx.enter_context(tc.tile_pool(name="scr", bufs=2))
+        psum_t = ctx.enter_context(tc.psum_pool(name="psum_t", bufs=3))
+        psum_h = ctx.enter_context(tc.psum_pool(name="psum_h", bufs=3))
+        psum_s = ctx.enter_context(tc.psum_pool(name="psum_s", bufs=1))
+
+        x_view = x_t.rearrange("(p j) k -> p j k", j=TILES)
+        h_view = h_prev.rearrange("(p j) k -> p j k", j=TILES)
+        x_sb = []
+        h_sb = []
+
+        def load_chunk(c):
+            tiles = slice(c * TPC, (c + 1) * TPC)
+            x_in = resident.tile([P, TPC * O], BF16, name="x_in")
+            nc.sync.dma_start(out=x_in.rearrange("p (j k) -> p j k", j=TPC), in_=x_view[:, tiles, :])
+            h_in = resident.tile([P, TPC * H], BF16, name="h_in")
+            nc.sync.dma_start(out=h_in.rearrange("p (j k) -> p j k", j=TPC), in_=h_view[:, tiles, :])
+            x_sb.append(x_in)
+            h_sb.append(h_in)
+
+        eps_sb = []
+        mup_sb = []
+        lvp_sb = []
+
+        def load_prior(half):
+            tiles = slice(half * HALF_TILES, (half + 1) * HALF_TILES)
+            for dram, keep, label in ((logvar_p, lvp_sb, "lvp"), (mu_p, mup_sb, "mup"), (eps, eps_sb, "eps")):
+                t = prior.tile([P, HALF_TILES, Z], BF16, name=label)
+                nc.sync.dma_start(out=t, in_=dram.rearrange("(p j) z -> p j z", j=TILES)[:, tiles, :])
+                keep.append(t)
+
+        w1_sb = const.tile([P, H_TILES * (O + H)], BF16, name="w1_sb")
+        nc.sync.dma_start(
+            out=w1_sb.rearrange("p (t k) -> p t k", t=H_TILES),
+            in_=enc_w1.rearrange("(p t) k -> p t k", t=H_TILES),
+        )
+        load_chunk(0)
+        w2_sb = const.tile([P, 2 * H], BF16, name="w2_sb")
+        nc.scalar.dma_start(
+            out=w2_sb.rearrange("p (a k) -> p a k", a=2), in_=enc_w2.rearrange("(a p) k -> p a k", p=P)
+        )
+        b1_sb = const.tile([P, H_TILES], BF16, name="b1_sb")
+        nc.scalar.dma_start(out=b1_sb, in_=enc_b1.rearrange("(p t) -> p t", t=H_TILES))
+        b2_bc = const.tile([P, 2 * Z], BF16, name="b2_bc")
+        nc.scalar.dma_start(out=b2_bc, in_=enc_b2.partition_broadcast(P))
+        load_chunk(1)
+        load_prior(0)
+        for c in range(2, NCH // 2 + 1):
+            load_chunk(c)
+        load_prior(1)
+        for c in range(NCH // 2 + 1, NCH):
+            load_chunk(c)
+
+        ident = const.tile([P, P], F32, name="ident")
+        make_identity(nc, ident)
+
+        w1_words = w1_sb.bitcast(F32)
+        w1_g = const.tile([P, 2 * H_TILES * P * PACK], BF16, name="w1_g", align_bytes=64)
+        w1_g_words = w1_g.bitcast(F32)
+        for g in range(2):
+            for a in range(2):
+                starts = [[(2 * a + s) * 2 * WORDS + g * WORDS + u * P for u in range(2)] for s in range(2)]
+                blocks = [[w1_words[:, w : w + P] for w in row] for row in starts]
+                bank = psum_t.tile([P, 2, 2 * P], F32, name="bank")
+                first = (g * H_TILES + 2 * a) * 2 * P
+                words_onto_partitions(
+                    nc, bank, ident, blocks, w1_g_words[:, first : first + 4 * P], nc.vector.tensor_copy
+                )
+        w1_c = const.tile([P, 2 * H_TILES * P], U32, name="w1_c", align_bytes=64)
+        w1_s = const.tile([P, 2 * H_TILES * P], U8, name="w1_s", align_bytes=64)
+        nc.vector.quantize_mx(out=w1_c.bitcast(FP8X4), scales=w1_s, in_=w1_g)
+
+        w2_words = w2_sb.bitcast(F32).rearrange("p (a w u) -> p a u w", a=2, u=2)
+        w2_g = const.tile([P, 2 * Z * PACK], BF16, name="w2_g", align_bytes=64)
+        bank = psum_t.tile([P, 2, 2 * P], F32, name="bank")
+        words_onto_partitions(
+            nc,
+            bank,
+            ident,
+            [[w2_words[:, a, u, :] for u in range(2)] for a in range(2)],
+            w2_g.bitcast(F32),
+            nc.vector.tensor_copy,
+        )
+        w2_c = const.tile([P, 2 * Z], U32, name="w2_c", align_bytes=64)
+        w2_s = const.tile([P, 2 * Z], U8, name="w2_s", align_bytes=64)
+        nc.vector.quantize_mx(out=w2_c.bitcast(FP8X4), scales=w2_s, in_=w2_g)
+
+        b1_f = const.tile([P, H_TILES], F32, name="b1_f")
+        nc.vector.tensor_copy(out=b1_f, in_=b1_sb)
+
+        sum_sq = const.tile([P, TILES], F32, name="sum_sq")
+        sum_ex = const.tile([P, TILES], F32, name="sum_ex")
+        sum_df = const.tile([P, TILES], F32, name="sum_df")
+
+        x_codes = {}
+        h_codes = {}
+        stats = {}
+
+        def quantise_inputs(c):
+            x_g = xq.tile([P, 2 * CHUNK * PACK], BF16, name="x_g", align_bytes=64)
+            x_g_words = x_g.bitcast(F32)
+            for g, src in enumerate((x_sb[c], h_sb[c])):
+                src_words = src.bitcast(F32)
+                for a in range(2):
+                    starts = [[(2 * a + s) * WORDS + u * P for u in range(2)] for s in range(2)]
+                    blocks = [[src_words[:, w : w + P] for w in row] for row in starts]
+                    bank = psum_t.tile([P, 2, 2 * P], F32, name="bank")
+                    first = g * 2 * CHUNK + a * 4 * P
+                    words_onto_partitions(
+                        nc, bank, ident, blocks, x_g_words[:, first : first + 4 * P], nc.scalar.copy
+                    )
+            x_c = xq.tile([P, 2 * CHUNK], U32, name="x_c", align_bytes=64)
+            x_s = xq.tile([P, 2 * CHUNK], U8, name="x_s", align_bytes=64)
+            nc.vector.quantize_mx(out=x_c.bitcast(FP8X4), scales=x_s, in_=x_g)
+            x_codes[c] = (x_c, x_s)
+
+        def hidden_layer(c):
+            x_c, x_s = x_codes[c]
+            h_b = hq.tile([P, H_TILES, CHUNK], BF16, name="h_b")
+            for t in range(H_TILES):
+                acc = psum_h.tile([P, CHUNK], F32, name="acc")
+                for g in range(2):
+                    w_cols = slice((g * H_TILES + t) * P, (g * H_TILES + t + 1) * P)
+                    x_cols = slice(g * CHUNK, (g + 1) * CHUNK)
+                    nc.tensor.matmul_mx(
+                        out=acc,
+                        lhsT=w1_c[:, w_cols].bitcast(FP8X4),
+                        lhsT_scale=w1_s[:, w_cols],
+                        rhs=x_c[:, x_cols].bitcast(FP8X4),
+                        rhs_scale=x_s[:, x_cols],
+                        start=(g == 0),
+                        stop=(g == 1),
+                    )
+                nc.scalar.activation(out=h_b[:, t, :], in_=acc, func=ACT.Relu, bias=b1_f[:, t : t + 1])
+            h_g = hq.tile([P, CHUNK * PACK], BF16, name="h_g", align_bytes=64)
+            nc.vector.tensor_copy(
+                out=h_g.rearrange("p (c i t) -> p c t i", i=4, t=PACK),
+                in_=h_b.rearrange("p t (c i) -> p c t i", i=4),
+            )
+            h_c = hq.tile([P, CHUNK], U32, name="h_c", align_bytes=64)
+            h_s = hq.tile([P, CHUNK], U8, name="h_s", align_bytes=64)
+            nc.vector.quantize_mx(out=h_c.bitcast(FP8X4), scales=h_s, in_=h_g)
+            h_codes[c] = (h_c, h_s)
+
+        def stats_layer(c):
+            h_c, h_s = h_codes[c]
+            st_mu = psum_s.tile([P, TPC, Z], F32, name="st_mu")
+            st_lv = psum_s.tile([P, TPC, Z], F32, name="st_lv")
+            for j in range(TPC):
+                tok = slice(j * P, (j + 1) * P)
+                for part, dst in enumerate((st_mu, st_lv)):
+                    cols = slice(part * Z, (part + 1) * Z)
+                    nc.tensor.matmul_mx(
+                        out=dst[:, j, :],
+                        lhsT=h_c[:, tok].bitcast(FP8X4),
+                        lhsT_scale=h_s[:, tok],
+                        rhs=w2_c[:, cols].bitcast(FP8X4),
+                        rhs_scale=w2_s[:, cols],
+                        start=True,
+                        stop=True,
+                    )
+            tiles = slice(c * TPC, (c + 1) * TPC)
+            local = slice((c * TPC) % HALF_TILES, (c * TPC) % HALF_TILES + TPC)
+            half = (c * TPC) // HALF_TILES
+            lvp = lvp_sb[half][:, local, :]
+            mup = mup_sb[half][:, local, :]
+
+            mu = outp.tile([P, TPC, Z], F32, name="mu")
+            nc.vector.tensor_tensor(
+                out=mu, in0=st_mu, in1=b2_bc[:, 0:Z].unsqueeze(1).to_broadcast([P, TPC, Z]), op=ALU.add
+            )
+            lv_raw = scr.tile([P, TPC, Z], F32, name="lv_raw")
+            nc.vector.tensor_tensor(
+                out=lv_raw, in0=st_lv, in1=b2_bc[:, Z : 2 * Z].unsqueeze(1).to_broadcast([P, TPC, Z]), op=ALU.add
+            )
+            lv = outp.tile([P, TPC, Z], F32, name="lv")
+            nc.vector.tensor_scalar(out=lv, in0=lv_raw, scalar1=-CLAMP, scalar2=CLAMP, op0=ALU.max, op1=ALU.min)
+            nc.sync.dma_start(out=mu_out.rearrange("(p j) z -> p j z", j=TILES)[:, tiles, :], in_=mu)
+            nc.sync.dma_start(out=lv_out.rearrange("(p j) z -> p j z", j=TILES)[:, tiles, :], in_=lv)
+
+            std = scr.tile([P, TPC, Z], F32, name="std")
+            nc.scalar.activation(out=std, in_=lv, func=ACT.Exp, scale=0.5)
+            inv_sd_p = scr.tile([P, TPC, Z], F32, name="inv_sd_p")
+            nc.scalar.activation(out=inv_sd_p, in_=lvp, func=ACT.Exp, scale=-0.5)
+
+            diff = scr.tile([P, TPC, Z], F32, name="diff")
+            nc.vector.tensor_tensor(out=diff, in0=mu, in1=mup, op=ALU.subtract)
+            ratio = scr.tile([P, TPC, Z], F32, name="ratio")
+            nc.vector.tensor_tensor(out=ratio, in0=diff, in1=inv_sd_p, op=ALU.mult)
+            dlv = scr.tile([P, TPC, Z], F32, name="dlv")
+            sq_junk = scr.tile([P, TPC, Z], BF16, name="sq_junk")
+            ex_junk = scr.tile([P, TPC, Z], BF16, name="ex_junk")
+            for j in range(TPC):
+                col = slice(c * TPC + j, c * TPC + j + 1)
+                nc.vector.scalar_tensor_tensor(
+                    out=dlv[:, j, :],
+                    in0=lv[:, j, :],
+                    scalar=1.0,
+                    in1=lvp[:, j, :],
+                    op0=ALU.mult,
+                    op1=ALU.subtract,
+                    accum_out=sum_df[:, col],
+                )
+            for j in range(TPC):
+                col = slice(c * TPC + j, c * TPC + j + 1)
+                nc.scalar.activation(
+                    out=sq_junk[:, j, :], in_=ratio[:, j, :], func=ACT.Square, accum_out=sum_sq[:, col]
+                )
+            for j in range(TPC):
+                col = slice(c * TPC + j, c * TPC + j + 1)
+                nc.scalar.activation(
+                    out=ex_junk[:, j, :], in_=dlv[:, j, :], func=ACT.Exp, accum_out=sum_ex[:, col]
+                )
+            stats[c] = (mu, std)
+
+        def sample(c):
+            mu, std = stats[c]
+            tiles = slice(c * TPC, (c + 1) * TPC)
+            local = slice((c * TPC) % HALF_TILES, (c * TPC) % HALF_TILES + TPC)
+            half = (c * TPC) // HALF_TILES
+            noise = scr.tile([P, TPC, Z], F32, name="noise")
+            nc.vector.tensor_tensor(out=noise, in0=std, in1=eps_sb[half][:, local, :], op=ALU.mult)
+            z = outp.tile([P, TPC, Z], F32, name="z")
+            nc.vector.tensor_tensor(out=z, in0=noise, in1=mu, op=ALU.add)
+            nc.sync.dma_start(out=z_out.rearrange("(p j) z -> p j z", j=TILES)[:, tiles, :], in_=z)
+
+        for c in range(NCH):
+            quantise_inputs(c)
+            hidden_layer(c)
+            stats_layer(c)
+            sample(c)
+
+        total = const.tile([P, TILES], F32, name="total")
+        nc.vector.tensor_tensor(out=total, in0=sum_sq, in1=sum_ex, op=ALU.add)
+        total2 = const.tile([P, TILES], F32, name="total2")
+        nc.vector.tensor_tensor(out=total2, in0=total, in1=sum_df, op=ALU.subtract)
+        kl = const.tile([P, TILES], F32, name="kl")
+        nc.vector.tensor_scalar(out=kl, in0=total2, scalar1=0.5, scalar2=-0.5 * Z, op0=ALU.mult, op1=ALU.add)
+        nc.sync.dma_start(out=kl_out.rearrange("(p j) -> p j", j=TILES), in_=kl)

@@ -24,17 +24,19 @@ NCH = TILES // TPC
 HALF_TILES = TILES // 2
 H_TILES = H // P
 
+LEAD = 3
+
 FLOPS = 2 * B * (O + H) * H + 2 * B * H * 2 * Z
 
 
-def words_onto_partitions(nc, bank, ident, word_blocks, grouped_words, copy):
+def transpose_words(nc, bank, ident, word_blocks):
     for s in range(2):
         for u in range(2):
             nc.tensor.transpose(bank[:, u, s * P : (s + 1) * P], word_blocks[s][u], ident)
-    copy(
-        out=grouped_words.rearrange("p (c u) -> p c u", u=2),
-        in_=bank.rearrange("p u c -> p c u"),
-    )
+
+
+def copy_grouped(copy, bank, grouped_words):
+    copy(out=grouped_words.rearrange("p (c u) -> p c u", u=2), in_=bank.rearrange("p u c -> p c u"))
 
 
 def tile_vrnncell_pa_t_kernel(
@@ -42,6 +44,7 @@ def tile_vrnncell_pa_t_kernel(
 ):
     nc = tc.nc
     with ExitStack() as ctx:
+        ctx.enter_context(tc.manual_schedule())
         const = ctx.enter_context(tc.tile_pool(name="const", bufs=1))
         resident = ctx.enter_context(tc.tile_pool(name="resident", bufs=NCH))
         prior = ctx.enter_context(tc.tile_pool(name="prior", bufs=2))
@@ -49,21 +52,25 @@ def tile_vrnncell_pa_t_kernel(
         hq = ctx.enter_context(tc.tile_pool(name="hq", bufs=2))
         outp = ctx.enter_context(tc.tile_pool(name="outp", bufs=3))
         scr = ctx.enter_context(tc.tile_pool(name="scr", bufs=2))
-        psum_t = ctx.enter_context(tc.psum_pool(name="psum_t", bufs=3))
-        psum_h = ctx.enter_context(tc.psum_pool(name="psum_h", bufs=3))
+        psum_t = ctx.enter_context(tc.psum_pool(name="psum_t", bufs=LEAD))
+        psum_h = ctx.enter_context(tc.psum_pool(name="psum_h", bufs=LEAD))
         psum_s = ctx.enter_context(tc.psum_pool(name="psum_s", bufs=1))
 
-        x_view = x_t.rearrange("(p j) k -> p j k", j=TILES)
-        h_view = h_prev.rearrange("(p j) k -> p j k", j=TILES)
+        def by_tile(dram):
+            return dram.rearrange("(p j) z -> p j z", j=TILES)
+
+        def live(c):
+            return 0 <= c < NCH
+
         x_sb = []
         h_sb = []
 
         def load_chunk(c):
             tiles = slice(c * TPC, (c + 1) * TPC)
             x_in = resident.tile([P, TPC * O], BF16, name="x_in")
-            nc.sync.dma_start(out=x_in.rearrange("p (j k) -> p j k", j=TPC), in_=x_view[:, tiles, :])
+            nc.sync.dma_start(out=x_in.rearrange("p (j k) -> p j k", j=TPC), in_=by_tile(x_t)[:, tiles, :])
             h_in = resident.tile([P, TPC * H], BF16, name="h_in")
-            nc.sync.dma_start(out=h_in.rearrange("p (j k) -> p j k", j=TPC), in_=h_view[:, tiles, :])
+            nc.sync.dma_start(out=h_in.rearrange("p (j k) -> p j k", j=TPC), in_=by_tile(h_prev)[:, tiles, :])
             x_sb.append(x_in)
             h_sb.append(h_in)
 
@@ -75,8 +82,12 @@ def tile_vrnncell_pa_t_kernel(
             tiles = slice(half * HALF_TILES, (half + 1) * HALF_TILES)
             for dram, keep, label in ((logvar_p, lvp_sb, "lvp"), (mu_p, mup_sb, "mup"), (eps, eps_sb, "eps")):
                 t = prior.tile([P, HALF_TILES, Z], BF16, name=label)
-                nc.sync.dma_start(out=t, in_=dram.rearrange("(p j) z -> p j z", j=TILES)[:, tiles, :])
+                nc.sync.dma_start(out=t, in_=by_tile(dram)[:, tiles, :])
                 keep.append(t)
+
+        def of_chunk(halves, c):
+            first = (c * TPC) % HALF_TILES
+            return halves[(c * TPC) // HALF_TILES][:, first : first + TPC, :]
 
         w1_sb = const.tile([P, H_TILES * (O + H)], BF16, name="w1_sb")
         nc.sync.dma_start(
@@ -109,175 +120,243 @@ def tile_vrnncell_pa_t_kernel(
         for g in range(2):
             for a in range(2):
                 starts = [[(2 * a + s) * 2 * WORDS + g * WORDS + u * P for u in range(2)] for s in range(2)]
-                blocks = [[w1_words[:, w : w + P] for w in row] for row in starts]
                 bank = psum_t.tile([P, 2, 2 * P], F32, name="bank")
+                transpose_words(nc, bank, ident, [[w1_words[:, w : w + P] for w in row] for row in starts])
                 first = (g * H_TILES + 2 * a) * 2 * P
-                words_onto_partitions(
-                    nc, bank, ident, blocks, w1_g_words[:, first : first + 4 * P], nc.vector.tensor_copy
-                )
+                copy = nc.vector.tensor_copy if a == 0 else nc.scalar.copy
+                copy_grouped(copy, bank, w1_g_words[:, first : first + 4 * P])
         w1_c = const.tile([P, 2 * H_TILES * P], U32, name="w1_c", align_bytes=64)
         w1_s = const.tile([P, 2 * H_TILES * P], U8, name="w1_s", align_bytes=64)
         nc.vector.quantize_mx(out=w1_c.bitcast(FP8X4), scales=w1_s, in_=w1_g)
-
-        w2_words = w2_sb.bitcast(F32).rearrange("p (a w u) -> p a u w", a=2, u=2)
-        w2_g = const.tile([P, 2 * Z * PACK], BF16, name="w2_g", align_bytes=64)
-        bank = psum_t.tile([P, 2, 2 * P], F32, name="bank")
-        words_onto_partitions(
-            nc,
-            bank,
-            ident,
-            [[w2_words[:, a, u, :] for u in range(2)] for a in range(2)],
-            w2_g.bitcast(F32),
-            nc.vector.tensor_copy,
-        )
-        w2_c = const.tile([P, 2 * Z], U32, name="w2_c", align_bytes=64)
-        w2_s = const.tile([P, 2 * Z], U8, name="w2_s", align_bytes=64)
-        nc.vector.quantize_mx(out=w2_c.bitcast(FP8X4), scales=w2_s, in_=w2_g)
-
         b1_f = const.tile([P, H_TILES], F32, name="b1_f")
         nc.vector.tensor_copy(out=b1_f, in_=b1_sb)
 
-        sum_sq = const.tile([P, TILES], F32, name="sum_sq")
-        sum_ex = const.tile([P, TILES], F32, name="sum_ex")
-        sum_df = const.tile([P, TILES], F32, name="sum_df")
+        banks = {}
+        x_g = {}
+        x_q = {}
 
-        x_codes = {}
-        h_codes = {}
-        stats = {}
+        def fill_bank(n):
+            c, g, a = n // 4, (n % 4) // 2, n % 2
+            src_words = (x_sb[c], h_sb[c])[g].bitcast(F32)
+            starts = [[(2 * a + s) * WORDS + u * P for u in range(2)] for s in range(2)]
+            banks[n] = psum_t.tile([P, 2, 2 * P], F32, name="bank")
+            transpose_words(nc, banks[n], ident, [[src_words[:, w : w + P] for w in row] for row in starts])
+
+        def empty_bank(n):
+            c = n // 4
+            if n % 4 == 0:
+                x_g[c] = xq.tile([P, 2 * CHUNK * PACK], BF16, name="x_g", align_bytes=64)
+            first = (n % 4) * 4 * P
+            copy_grouped(nc.scalar.copy, banks[n], x_g[c].bitcast(F32)[:, first : first + 4 * P])
 
         def quantise_inputs(c):
-            x_g = xq.tile([P, 2 * CHUNK * PACK], BF16, name="x_g", align_bytes=64)
-            x_g_words = x_g.bitcast(F32)
-            for g, src in enumerate((x_sb[c], h_sb[c])):
-                src_words = src.bitcast(F32)
-                for a in range(2):
-                    starts = [[(2 * a + s) * WORDS + u * P for u in range(2)] for s in range(2)]
-                    blocks = [[src_words[:, w : w + P] for w in row] for row in starts]
-                    bank = psum_t.tile([P, 2, 2 * P], F32, name="bank")
-                    first = g * 2 * CHUNK + a * 4 * P
-                    words_onto_partitions(
-                        nc, bank, ident, blocks, x_g_words[:, first : first + 4 * P], nc.scalar.copy
-                    )
-            x_c = xq.tile([P, 2 * CHUNK], U32, name="x_c", align_bytes=64)
-            x_s = xq.tile([P, 2 * CHUNK], U8, name="x_s", align_bytes=64)
-            nc.vector.quantize_mx(out=x_c.bitcast(FP8X4), scales=x_s, in_=x_g)
-            x_codes[c] = (x_c, x_s)
+            codes = xq.tile([P, 2 * CHUNK], U32, name="x_codes", align_bytes=64)
+            scales = xq.tile([P, 2 * CHUNK], U8, name="x_scales", align_bytes=64)
+            for g in range(2):
+                cols = slice(g * CHUNK, (g + 1) * CHUNK)
+                nc.vector.quantize_mx(
+                    out=codes[:, cols].bitcast(FP8X4),
+                    scales=scales[:, cols],
+                    in_=x_g[c][:, g * CHUNK * PACK : (g + 1) * CHUNK * PACK],
+                )
+            x_q[c] = (codes, scales)
 
-        def hidden_layer(c):
-            x_c, x_s = x_codes[c]
-            h_b = hq.tile([P, H_TILES, CHUNK], BF16, name="h_b")
-            for t in range(H_TILES):
-                acc = psum_h.tile([P, CHUNK], F32, name="acc")
-                for g in range(2):
-                    w_cols = slice((g * H_TILES + t) * P, (g * H_TILES + t + 1) * P)
-                    x_cols = slice(g * CHUNK, (g + 1) * CHUNK)
-                    nc.tensor.matmul_mx(
-                        out=acc,
-                        lhsT=w1_c[:, w_cols].bitcast(FP8X4),
-                        lhsT_scale=w1_s[:, w_cols],
-                        rhs=x_c[:, x_cols].bitcast(FP8X4),
-                        rhs_scale=x_s[:, x_cols],
-                        start=(g == 0),
-                        stop=(g == 1),
-                    )
-                nc.scalar.activation(out=h_b[:, t, :], in_=acc, func=ACT.Relu, bias=b1_f[:, t : t + 1])
-            h_g = hq.tile([P, CHUNK * PACK], BF16, name="h_g", align_bytes=64)
+        accs = {}
+        h_b = {}
+        h_g = {}
+        h_q = {}
+
+        def hidden_group(c, t):
+            codes, scales = x_q[c]
+            accs[(c, t)] = psum_h.tile([P, CHUNK], F32, name="acc")
+            for g in range(2):
+                w_cols = slice((g * H_TILES + t) * P, (g * H_TILES + t + 1) * P)
+                x_cols = slice(g * CHUNK, (g + 1) * CHUNK)
+                nc.tensor.matmul_mx(
+                    out=accs[(c, t)],
+                    lhsT=w1_c[:, w_cols].bitcast(FP8X4),
+                    lhsT_scale=w1_s[:, w_cols],
+                    rhs=codes[:, x_cols].bitcast(FP8X4),
+                    rhs_scale=scales[:, x_cols],
+                    start=(g == 0),
+                    stop=(g == 1),
+                )
+
+        def relu_group(c, t):
+            if t == 0:
+                h_b[c] = hq.tile([P, H_TILES, CHUNK], BF16, name="h_b")
+            nc.scalar.activation(out=h_b[c][:, t, :], in_=accs[(c, t)], func=ACT.Relu, bias=b1_f[:, t : t + 1])
+
+        def regroup_hidden(c):
+            h_g[c] = hq.tile([P, CHUNK * PACK], BF16, name="h_g", align_bytes=64)
             nc.vector.tensor_copy(
-                out=h_g.rearrange("p (c i t) -> p c t i", i=4, t=PACK),
-                in_=h_b.rearrange("p t (c i) -> p c t i", i=4),
+                out=h_g[c].rearrange("p (c i t) -> p c t i", i=4, t=PACK),
+                in_=h_b[c].rearrange("p t (c i) -> p c t i", i=4),
             )
-            h_c = hq.tile([P, CHUNK], U32, name="h_c", align_bytes=64)
-            h_s = hq.tile([P, CHUNK], U8, name="h_s", align_bytes=64)
-            nc.vector.quantize_mx(out=h_c.bitcast(FP8X4), scales=h_s, in_=h_g)
-            h_codes[c] = (h_c, h_s)
 
-        def stats_layer(c):
-            h_c, h_s = h_codes[c]
-            st_mu = psum_s.tile([P, TPC, Z], F32, name="st_mu")
-            st_lv = psum_s.tile([P, TPC, Z], F32, name="st_lv")
+        def quantise_hidden(c):
+            codes = hq.tile([P, CHUNK], U32, name="h_codes", align_bytes=64)
+            scales = hq.tile([P, CHUNK], U8, name="h_scales", align_bytes=64)
+            nc.vector.quantize_mx(out=codes.bitcast(FP8X4), scales=scales, in_=h_g[c])
+            h_q[c] = (codes, scales)
+
+        st_mu = {}
+        st_lv = {}
+
+        def stats_matmuls(c):
+            codes, scales = h_q[c]
+            st_mu[c] = psum_s.tile([P, TPC, Z], F32, name="st_mu")
+            st_lv[c] = psum_s.tile([P, TPC, Z], F32, name="st_lv")
             for j in range(TPC):
                 tok = slice(j * P, (j + 1) * P)
-                for part, dst in enumerate((st_mu, st_lv)):
+                for part, dst in enumerate((st_mu[c], st_lv[c])):
                     cols = slice(part * Z, (part + 1) * Z)
                     nc.tensor.matmul_mx(
                         out=dst[:, j, :],
-                        lhsT=h_c[:, tok].bitcast(FP8X4),
-                        lhsT_scale=h_s[:, tok],
+                        lhsT=codes[:, tok].bitcast(FP8X4),
+                        lhsT_scale=scales[:, tok],
                         rhs=w2_c[:, cols].bitcast(FP8X4),
                         rhs_scale=w2_s[:, cols],
                         start=True,
                         stop=True,
                     )
-            tiles = slice(c * TPC, (c + 1) * TPC)
-            local = slice((c * TPC) % HALF_TILES, (c * TPC) % HALF_TILES + TPC)
-            half = (c * TPC) // HALF_TILES
-            lvp = lvp_sb[half][:, local, :]
-            mup = mup_sb[half][:, local, :]
 
-            mu = outp.tile([P, TPC, Z], F32, name="mu")
-            nc.vector.tensor_tensor(
-                out=mu, in0=st_mu, in1=b2_bc[:, 0:Z].unsqueeze(1).to_broadcast([P, TPC, Z]), op=ALU.add
+        def chunk_tile(pool, label, dtype=F32):
+            return pool.tile([P, TPC, Z], dtype, name=label)
+
+        def store(dram, c, tile):
+            nc.sync.dma_start(out=by_tile(dram)[:, c * TPC : (c + 1) * TPC, :], in_=tile)
+
+        def bias_of(part):
+            return b2_bc[:, part * Z : (part + 1) * Z].unsqueeze(1).to_broadcast([P, TPC, Z])
+
+        mu = {}
+        lv_raw = {}
+        lv = {}
+        std = {}
+        inv_sd_p = {}
+        diff = {}
+        ratio = {}
+        dlv = {}
+        noise = {}
+        sum_sq = const.tile([P, TILES], F32, name="sum_sq")
+        sum_ex = const.tile([P, TILES], F32, name="sum_ex")
+        sum_df = const.tile([P, TILES], F32, name="sum_df")
+
+        def add_bias_mean(c):
+            mu[c] = chunk_tile(outp, "mu")
+            nc.vector.tensor_tensor(out=mu[c], in0=st_mu[c], in1=bias_of(0), op=ALU.add)
+            store(mu_out, c, mu[c])
+
+        def add_bias_logvar(c):
+            lv_raw[c] = chunk_tile(scr, "lv_raw")
+            nc.vector.tensor_tensor(out=lv_raw[c], in0=st_lv[c], in1=bias_of(1), op=ALU.add)
+
+        def clip_logvar(c):
+            lv[c] = chunk_tile(outp, "lv")
+            nc.vector.tensor_scalar(
+                out=lv[c], in0=lv_raw[c], scalar1=-CLAMP, scalar2=CLAMP, op0=ALU.max, op1=ALU.min
             )
-            lv_raw = scr.tile([P, TPC, Z], F32, name="lv_raw")
-            nc.vector.tensor_tensor(
-                out=lv_raw, in0=st_lv, in1=b2_bc[:, Z : 2 * Z].unsqueeze(1).to_broadcast([P, TPC, Z]), op=ALU.add
-            )
-            lv = outp.tile([P, TPC, Z], F32, name="lv")
-            nc.vector.tensor_scalar(out=lv, in0=lv_raw, scalar1=-CLAMP, scalar2=CLAMP, op0=ALU.max, op1=ALU.min)
-            nc.sync.dma_start(out=mu_out.rearrange("(p j) z -> p j z", j=TILES)[:, tiles, :], in_=mu)
-            nc.sync.dma_start(out=lv_out.rearrange("(p j) z -> p j z", j=TILES)[:, tiles, :], in_=lv)
+            store(lv_out, c, lv[c])
 
-            std = scr.tile([P, TPC, Z], F32, name="std")
-            nc.scalar.activation(out=std, in_=lv, func=ACT.Exp, scale=0.5)
-            inv_sd_p = scr.tile([P, TPC, Z], F32, name="inv_sd_p")
-            nc.scalar.activation(out=inv_sd_p, in_=lvp, func=ACT.Exp, scale=-0.5)
+        def mean_difference(c):
+            diff[c] = chunk_tile(scr, "diff")
+            nc.vector.tensor_tensor(out=diff[c], in0=mu[c], in1=of_chunk(mup_sb, c), op=ALU.subtract)
 
-            diff = scr.tile([P, TPC, Z], F32, name="diff")
-            nc.vector.tensor_tensor(out=diff, in0=mu, in1=mup, op=ALU.subtract)
-            ratio = scr.tile([P, TPC, Z], F32, name="ratio")
-            nc.vector.tensor_tensor(out=ratio, in0=diff, in1=inv_sd_p, op=ALU.mult)
-            dlv = scr.tile([P, TPC, Z], F32, name="dlv")
-            sq_junk = scr.tile([P, TPC, Z], BF16, name="sq_junk")
-            ex_junk = scr.tile([P, TPC, Z], BF16, name="ex_junk")
+        def scale_difference(c):
+            ratio[c] = chunk_tile(scr, "ratio")
+            nc.vector.tensor_tensor(out=ratio[c], in0=diff[c], in1=inv_sd_p[c], op=ALU.mult)
+
+        def logvar_difference(c):
+            dlv[c] = chunk_tile(scr, "dlv")
             for j in range(TPC):
-                col = slice(c * TPC + j, c * TPC + j + 1)
                 nc.vector.scalar_tensor_tensor(
-                    out=dlv[:, j, :],
-                    in0=lv[:, j, :],
+                    out=dlv[c][:, j, :],
+                    in0=lv[c][:, j, :],
                     scalar=1.0,
-                    in1=lvp[:, j, :],
+                    in1=of_chunk(lvp_sb, c)[:, j, :],
                     op0=ALU.mult,
                     op1=ALU.subtract,
-                    accum_out=sum_df[:, col],
+                    accum_out=sum_df[:, c * TPC + j : c * TPC + j + 1],
                 )
-            for j in range(TPC):
-                col = slice(c * TPC + j, c * TPC + j + 1)
-                nc.scalar.activation(
-                    out=sq_junk[:, j, :], in_=ratio[:, j, :], func=ACT.Square, accum_out=sum_sq[:, col]
-                )
-            for j in range(TPC):
-                col = slice(c * TPC + j, c * TPC + j + 1)
-                nc.scalar.activation(
-                    out=ex_junk[:, j, :], in_=dlv[:, j, :], func=ACT.Exp, accum_out=sum_ex[:, col]
-                )
-            stats[c] = (mu, std)
 
-        def sample(c):
-            mu, std = stats[c]
-            tiles = slice(c * TPC, (c + 1) * TPC)
-            local = slice((c * TPC) % HALF_TILES, (c * TPC) % HALF_TILES + TPC)
-            half = (c * TPC) // HALF_TILES
-            noise = scr.tile([P, TPC, Z], F32, name="noise")
-            nc.vector.tensor_tensor(out=noise, in0=std, in1=eps_sb[half][:, local, :], op=ALU.mult)
-            z = outp.tile([P, TPC, Z], F32, name="z")
-            nc.vector.tensor_tensor(out=z, in0=noise, in1=mu, op=ALU.add)
-            nc.sync.dma_start(out=z_out.rearrange("(p j) z -> p j z", j=TILES)[:, tiles, :], in_=z)
+        def posterior_sd(c):
+            std[c] = chunk_tile(scr, "std")
+            nc.scalar.activation(out=std[c], in_=lv[c], func=ACT.Exp, scale=0.5)
 
-        for c in range(NCH):
-            quantise_inputs(c)
-            hidden_layer(c)
-            stats_layer(c)
-            sample(c)
+        def prior_inverse_sd(c):
+            inv_sd_p[c] = chunk_tile(scr, "inv_sd_p")
+            nc.scalar.activation(out=inv_sd_p[c], in_=of_chunk(lvp_sb, c), func=ACT.Exp, scale=-0.5)
+
+        def row_sums(c, func, values, sums, label):
+            unread = chunk_tile(scr, label, BF16)
+            for j in range(TPC):
+                nc.scalar.activation(
+                    out=unread[:, j, :],
+                    in_=values[:, j, :],
+                    func=func,
+                    accum_out=sums[:, c * TPC + j : c * TPC + j + 1],
+                )
+
+        def scale_noise(c):
+            noise[c] = chunk_tile(scr, "noise")
+            nc.vector.tensor_tensor(out=noise[c], in0=std[c], in1=of_chunk(eps_sb, c), op=ALU.mult)
+
+        def add_mean(c):
+            z = chunk_tile(outp, "z")
+            nc.vector.tensor_tensor(out=z, in0=noise[c], in1=mu[c], op=ALU.add)
+            store(z_out, c, z)
+
+        for n in range(LEAD):
+            fill_bank(n)
+
+        w2_words = w2_sb.bitcast(F32).rearrange("p (a w u) -> p a u w", a=2, u=2)
+        w2_g = const.tile([P, 2 * Z * PACK], BF16, name="w2_g", align_bytes=64)
+        w2_bank = psum_s.tile([P, 2, 2 * P], F32, name="w2_bank", tag="st_mu")
+        transpose_words(nc, w2_bank, ident, [[w2_words[:, a, u, :] for u in range(2)] for a in range(2)])
+        copy_grouped(nc.vector.tensor_copy, w2_bank, w2_g.bitcast(F32))
+        w2_c = const.tile([P, 2 * Z], U32, name="w2_c", align_bytes=64)
+        w2_s = const.tile([P, 2 * Z], U8, name="w2_s", align_bytes=64)
+        nc.vector.quantize_mx(out=w2_c.bitcast(FP8X4), scales=w2_s, in_=w2_g)
+
+        for i in range(NCH + 3):
+            if live(i - 1):
+                for t in range(H_TILES):
+                    relu_group(i - 1, t)
+                    if t + LEAD < H_TILES:
+                        hidden_group(i - 1, t + LEAD)
+            if live(i - 2):
+                add_bias_logvar(i - 2)
+                add_bias_mean(i - 2)
+                clip_logvar(i - 2)
+                mean_difference(i - 2)
+                logvar_difference(i - 2)
+                scale_difference(i - 2)
+            if live(i):
+                for q in range(4):
+                    empty_bank(4 * i + q)
+                    if 4 * i + q + LEAD < 4 * NCH:
+                        fill_bank(4 * i + q + LEAD)
+            if live(i - 1):
+                regroup_hidden(i - 1)
+            if live(i - 3):
+                scale_noise(i - 3)
+            if live(i - 1):
+                quantise_hidden(i - 1)
+                stats_matmuls(i - 1)
+            if live(i - 3):
+                add_mean(i - 3)
+            if live(i):
+                quantise_inputs(i)
+                for t in range(LEAD):
+                    hidden_group(i, t)
+            if live(i - 2):
+                posterior_sd(i - 2)
+            if live(i - 1):
+                prior_inverse_sd(i - 1)
+            if live(i - 2):
+                row_sums(i - 2, ACT.Exp, dlv[i - 2], sum_ex, "ex_unread")
+                row_sums(i - 2, ACT.Square, ratio[i - 2], sum_sq, "sq_unread")
 
         total = const.tile([P, TILES], F32, name="total")
         nc.vector.tensor_tensor(out=total, in0=sum_sq, in1=sum_ex, op=ALU.add)

@@ -24,6 +24,7 @@ NCH = TILES // TPC
 HALF_TILES = TILES // 2
 H_TILES = H // P
 
+VECTOR_COPIES = 1
 LEAD = 3
 
 FLOPS = 2 * B * (O + H) * H + 2 * B * H * 2 * Z
@@ -147,7 +148,8 @@ def tile_vrnncell_pa_t_kernel(
             if n % 4 == 0:
                 x_g[c] = xq.tile([P, 2 * CHUNK * PACK], BF16, name="x_g", align_bytes=64)
             first = (n % 4) * 4 * P
-            copy_grouped(nc.scalar.copy, banks[n], x_g[c].bitcast(F32)[:, first : first + 4 * P])
+            copy = nc.vector.tensor_copy if n % 4 < VECTOR_COPIES else nc.scalar.copy
+            copy_grouped(copy, banks[n], x_g[c].bitcast(F32)[:, first : first + 4 * P])
 
         def quantise_inputs(c):
             codes = xq.tile([P, 2 * CHUNK], U32, name="x_codes", align_bytes=64)

@@ -302,11 +302,11 @@ def tile_vrnncell_pa_t_kernel(
 
         def scale_noise(c):
             noise[c] = chunk_tile(scr, "noise")
-            nc.vector.tensor_tensor(out=noise[c], in0=std[c], in1=of_chunk(eps_sb, c), op=ALU.mult)
+            nc.gpsimd.tensor_tensor(out=noise[c], in0=std[c], in1=of_chunk(eps_sb, c), op=ALU.mult)
 
         def add_mean(c):
             z = chunk_tile(outp, "z")
-            nc.vector.tensor_tensor(out=z, in0=noise[c], in1=mu[c], op=ALU.add)
+            nc.gpsimd.tensor_tensor(out=z, in0=noise[c], in1=mu[c], op=ALU.add)
             store(z_out, c, z)
 
         for n in range(LEAD):

from contextlib import ExitStack

import concourse.mybir as mybir
from concourse.masks import make_identity

F32 = mybir.dt.float32
BF16 = mybir.dt.bfloat16
U32 = mybir.dt.uint32
U8 = mybir.dt.uint8
FP8X4 = mybir.dt.float8_e4m3fn_x4
ACT = mybir.ActivationFunctionType
ALU = mybir.AluOpType

P = 128
B, O, H, Z = 4096, 512, 512, 128
CLAMP = 10.0
PACK = 4
K_PASS = P * PACK
WORDS = K_PASS // 2
TILES = B // P
TPC = 4
CHUNK = TPC * P
NCH = TILES // TPC
HALF_TILES = TILES // 2
H_TILES = H // P

VECTOR_COPIES = 1
LEAD = 3

FLOPS = 2 * B * (O + H) * H + 2 * B * H * 2 * Z


def transpose_words(nc, bank, ident, word_blocks):
    for s in range(2):
        for u in range(2):
            nc.tensor.transpose(bank[:, u, s * P : (s + 1) * P], word_blocks[s][u], ident)


def copy_grouped(copy, bank, grouped_words):
    copy(out=grouped_words.rearrange("p (c u) -> p c u", u=2), in_=bank.rearrange("p u c -> p c u"))


def tile_vrnncell_pa_t_kernel(
    tc, x_t, h_prev, eps, enc_w1, enc_b1, enc_w2, enc_b2, mu_p, logvar_p, z_out, mu_out, lv_out, kl_out
):
    nc = tc.nc
    with ExitStack() as ctx:
        ctx.enter_context(tc.manual_schedule())
        const = ctx.enter_context(tc.tile_pool(name="const", bufs=1))
        resident = ctx.enter_context(tc.tile_pool(name="resident", bufs=NCH))
        prior = ctx.enter_context(tc.tile_pool(name="prior", bufs=2))
        xq = ctx.enter_context(tc.tile_pool(name="xq", bufs=2))
        hq = ctx.enter_context(tc.tile_pool(name="hq", bufs=2))
        outp = ctx.enter_context(tc.tile_pool(name="outp", bufs=3))
        scr = ctx.enter_context(tc.tile_pool(name="scr", bufs=2))
        psum_t = ctx.enter_context(tc.psum_pool(name="psum_t", bufs=LEAD))
        psum_h = ctx.enter_context(tc.psum_pool(name="psum_h", bufs=LEAD))
        psum_s = ctx.enter_context(tc.psum_pool(name="psum_s", bufs=1))

        def by_tile(dram):
            return dram.rearrange("(p j) z -> p j z", j=TILES)

        def live(c):
            return 0 <= c < NCH

        x_sb = []
        h_sb = []

        def load_chunk(c):
            tiles = slice(c * TPC, (c + 1) * TPC)
            x_in = resident.tile([P, TPC * O], BF16, name="x_in")
            nc.sync.dma_start(out=x_in.rearrange("p (j k) -> p j k", j=TPC), in_=by_tile(x_t)[:, tiles, :])
            h_in = resident.tile([P, TPC * H], BF16, name="h_in")
            nc.sync.dma_start(out=h_in.rearrange("p (j k) -> p j k", j=TPC), in_=by_tile(h_prev)[:, tiles, :])
            x_sb.append(x_in)
            h_sb.append(h_in)

        eps_sb = []
        mup_sb = []
        lvp_sb = []

        def load_prior(half):
            tiles = slice(half * HALF_TILES, (half + 1) * HALF_TILES)
            for dram, keep, label in ((logvar_p, lvp_sb, "lvp"), (mu_p, mup_sb, "mup"), (eps, eps_sb, "eps")):
                t = prior.tile([P, HALF_TILES, Z], BF16, name=label)
                nc.sync.dma_start(out=t, in_=by_tile(dram)[:, tiles, :])
                keep.append(t)

        def of_chunk(halves, c):
            first = (c * TPC) % HALF_TILES
            return halves[(c * TPC) // HALF_TILES][:, first : first + TPC, :]

        w1_sb = const.tile([P, H_TILES * (O + H)], BF16, name="w1_sb")
        nc.sync.dma_start(
            out=w1_sb.rearrange("p (t k) -> p t k", t=H_TILES),
            in_=enc_w1.rearrange("(p t) k -> p t k", t=H_TILES),
        )
        load_chunk(0)
        w2_sb = const.tile([P, 2 * H], BF16, name="w2_sb")
        nc.scalar.dma_start(
            out=w2_sb.rearrange("p (a k) -> p a k", a=2), in_=enc_w2.rearrange("(a p) k -> p a k", p=P)
        )
        b1_sb = const.tile([P, H_TILES], BF16, name="b1_sb")
        nc.scalar.dma_start(out=b1_sb, in_=enc_b1.rearrange("(p t) -> p t", t=H_TILES))
        b2_bc = const.tile([P, 2 * Z], BF16, name="b2_bc")
        nc.scalar.dma_start(out=b2_bc, in_=enc_b2.partition_broadcast(P))
        load_chunk(1)
        load_prior(0)
        for c in range(2, NCH // 2 + 1):
            load_chunk(c)
        load_prior(1)
        for c in range(NCH // 2 + 1, NCH):
            load_chunk(c)

        ident = const.tile([P, P], F32, name="ident")
        make_identity(nc, ident)

        w1_words = w1_sb.bitcast(F32)
        w1_g = const.tile([P, 2 * H_TILES * P * PACK], BF16, name="w1_g", align_bytes=64)
        w1_g_words = w1_g.bitcast(F32)
        for g in range(2):
            for a in range(2):
                starts = [[(2 * a + s) * 2 * WORDS + g * WORDS + u * P for u in range(2)] for s in range(2)]
                bank = psum_t.tile([P, 2, 2 * P], F32, name="bank")
                transpose_words(nc, bank, ident, [[w1_words[:, w : w + P] for w in row] for row in starts])
                first = (g * H_TILES + 2 * a) * 2 * P
                copy = nc.vector.tensor_copy if a == 0 else nc.scalar.copy
                copy_grouped(copy, bank, w1_g_words[:, first : first + 4 * P])
        w1_c = const.tile([P, 2 * H_TILES * P], U32, name="w1_c", align_bytes=64)
        w1_s = const.tile([P, 2 * H_TILES * P], U8, name="w1_s", align_bytes=64)
        nc.vector.quantize_mx(out=w1_c.bitcast(FP8X4), scales=w1_s, in_=w1_g)
        b1_f = const.tile([P, H_TILES], F32, name="b1_f")
        nc.vector.tensor_copy(out=b1_f, in_=b1_sb)

        banks = {}
        x_g = {}
        x_q = {}

        def fill_bank(n):
            c, g, a = n // 4, (n % 4) // 2, n % 2
            src_words = (x_sb[c], h_sb[c])[g].bitcast(F32)
            starts = [[(2 * a + s) * WORDS + u * P for u in range(2)] for s in range(2)]
            banks[n] = psum_t.tile([P, 2, 2 * P], F32, name="bank")
            transpose_words(nc, banks[n], ident, [[src_words[:, w : w + P] for w in row] for row in starts])

        def empty_bank(n):
            c = n // 4
            if n % 4 == 0:
                x_g[c] = xq.tile([P, 2 * CHUNK * PACK], BF16, name="x_g", align_bytes=64)
            first = (n % 4) * 4 * P
            copy = nc.vector.tensor_copy if n % 4 < VECTOR_COPIES else nc.scalar.copy
            copy_grouped(copy, banks[n], x_g[c].bitcast(F32)[:, first : first + 4 * P])

        def quantise_inputs(c):
            codes = xq.tile([P, 2 * CHUNK], U32, name="x_codes", align_bytes=64)
            scales = xq.tile([P, 2 * CHUNK], U8, name="x_scales", align_bytes=64)
            for g in range(2):
                cols = slice(g * CHUNK, (g + 1) * CHUNK)
                nc.vector.quantize_mx(
                    out=codes[:, cols].bitcast(FP8X4),
                    scales=scales[:, cols],
                    in_=x_g[c][:, g * CHUNK * PACK : (g + 1) * CHUNK * PACK],
                )
            x_q[c] = (codes, scales)

        accs = {}
        h_b = {}
        h_g = {}
        h_q = {}

        def hidden_group(c, t):
            codes, scales = x_q[c]
            accs[(c, t)] = psum_h.tile([P, CHUNK], F32, name="acc")
            for g in range(2):
                w_cols = slice((g * H_TILES + t) * P, (g * H_TILES + t + 1) * P)
                x_cols = slice(g * CHUNK, (g + 1) * CHUNK)
                nc.tensor.matmul_mx(
                    out=accs[(c, t)],
                    lhsT=w1_c[:, w_cols].bitcast(FP8X4),
                    lhsT_scale=w1_s[:, w_cols],
                    rhs=codes[:, x_cols].bitcast(FP8X4),
                    rhs_scale=scales[:, x_cols],
                    start=(g == 0),
                    stop=(g == 1),
                )

        def relu_group(c, t):
            if t == 0:
                h_b[c] = hq.tile([P, H_TILES, CHUNK], BF16, name="h_b")
            nc.scalar.activation(out=h_b[c][:, t, :], in_=accs[(c, t)], func=ACT.Relu, bias=b1_f[:, t : t + 1])

        def regroup_hidden(c):
            h_g[c] = hq.tile([P, CHUNK * PACK], BF16, name="h_g", align_bytes=64)
            nc.vector.tensor_copy(
                out=h_g[c].rearrange("p (c i t) -> p c t i", i=4, t=PACK),
                in_=h_b[c].rearrange("p t (c i) -> p c t i", i=4),
            )

        def quantise_hidden(c):
            codes = hq.tile([P, CHUNK], U32, name="h_codes", align_bytes=64)
            scales = hq.tile([P, CHUNK], U8, name="h_scales", align_bytes=64)
            nc.vector.quantize_mx(out=codes.bitcast(FP8X4), scales=scales, in_=h_g[c])
            h_q[c] = (codes, scales)

        st_mu = {}
        st_lv = {}

        def stats_matmuls(c):
            codes, scales = h_q[c]
            st_mu[c] = psum_s.tile([P, TPC, Z], F32, name="st_mu")
            st_lv[c] = psum_s.tile([P, TPC, Z], F32, name="st_lv")
            for j in range(TPC):
                tok = slice(j * P, (j + 1) * P)
                for part, dst in enumerate((st_mu[c], st_lv[c])):
                    cols = slice(part * Z, (part + 1) * Z)
                    nc.tensor.matmul_mx(
                        out=dst[:, j, :],
                        lhsT=codes[:, tok].bitcast(FP8X4),
                        lhsT_scale=scales[:, tok],
                        rhs=w2_c[:, cols].bitcast(FP8X4),
                        rhs_scale=w2_s[:, cols],
                        start=True,
                        stop=True,
                    )

        def chunk_tile(pool, label, dtype=F32):
            return pool.tile([P, TPC, Z], dtype, name=label)

        def store(dram, c, tile):
            nc.sync.dma_start(out=by_tile(dram)[:, c * TPC : (c + 1) * TPC, :], in_=tile)

        def bias_of(part):
            return b2_bc[:, part * Z : (part + 1) * Z].unsqueeze(1).to_broadcast([P, TPC, Z])

        mu = {}
        lv_raw = {}
        lv = {}
        std = {}
        inv_sd_p = {}
        diff = {}
        ratio = {}
        dlv = {}
        noise = {}
        sum_sq = const.tile([P, TILES], F32, name="sum_sq")
        sum_ex = const.tile([P, TILES], F32, name="sum_ex")
        sum_df = const.tile([P, TILES], F32, name="sum_df")

        def add_bias_mean(c):
            mu[c] = chunk_tile(outp, "mu")
            nc.vector.tensor_tensor(out=mu[c], in0=st_mu[c], in1=bias_of(0), op=ALU.add)
            store(mu_out, c, mu[c])

        def add_bias_logvar(c):
            lv_raw[c] = chunk_tile(scr, "lv_raw")
            nc.vector.tensor_tensor(out=lv_raw[c], in0=st_lv[c], in1=bias_of(1), op=ALU.add)

        def clip_logvar(c):
            lv[c] = chunk_tile(outp, "lv")
            nc.vector.tensor_scalar(
                out=lv[c], in0=lv_raw[c], scalar1=-CLAMP, scalar2=CLAMP, op0=ALU.max, op1=ALU.min
            )
            store(lv_out, c, lv[c])

        def mean_difference(c):
            diff[c] = chunk_tile(scr, "diff")
            nc.vector.tensor_tensor(out=diff[c], in0=mu[c], in1=of_chunk(mup_sb, c), op=ALU.subtract)

        def scale_difference(c):
            ratio[c] = chunk_tile(scr, "ratio")
            nc.vector.tensor_tensor(out=ratio[c], in0=diff[c], in1=inv_sd_p[c], op=ALU.mult)

        def logvar_difference(c):
            dlv[c] = chunk_tile(scr, "dlv")
            for j in range(TPC):
                nc.vector.scalar_tensor_tensor(
                    out=dlv[c][:, j, :],
                    in0=lv[c][:, j, :],
                    scalar=1.0,
                    in1=of_chunk(lvp_sb, c)[:, j, :],
                    op0=ALU.mult,
                    op1=ALU.subtract,
                    accum_out=sum_df[:, c * TPC + j : c * TPC + j + 1],
                )

        def posterior_sd(c):
            std[c] = chunk_tile(scr, "std")
            nc.scalar.activation(out=std[c], in_=lv[c], func=ACT.Exp, scale=0.5)

        def prior_inverse_sd(c):
            inv_sd_p[c] = chunk_tile(scr, "inv_sd_p")
            nc.scalar.activation(out=inv_sd_p[c], in_=of_chunk(lvp_sb, c), func=ACT.Exp, scale=-0.5)

        def row_sums(c, func, values, sums, label):
            unread = chunk_tile(scr, label, BF16)
            for j in range(TPC):
                nc.scalar.activation(
                    out=unread[:, j, :],
                    in_=values[:, j, :],
                    func=func,
                    accum_out=sums[:, c * TPC + j : c * TPC + j + 1],
                )

        def scale_noise(c):
            noise[c] = chunk_tile(scr, "noise")
            nc.gpsimd.tensor_tensor(out=noise[c], in0=std[c], in1=of_chunk(eps_sb, c), op=ALU.mult)

        def add_mean(c):
            z = chunk_tile(outp, "z")
            nc.gpsimd.tensor_tensor(out=z, in0=noise[c], in1=mu[c], op=ALU.add)
            store(z_out, c, z)

        for n in range(LEAD):
            fill_bank(n)

        w2_words = w2_sb.bitcast(F32).rearrange("p (a w u) -> p a u w", a=2, u=2)
        w2_g = const.tile([P, 2 * Z * PACK], BF16, name="w2_g", align_bytes=64)
        w2_bank = psum_s.tile([P, 2, 2 * P], F32, name="w2_bank", tag="st_mu")
        transpose_words(nc, w2_bank, ident, [[w2_words[:, a, u, :] for u in range(2)] for a in range(2)])
        copy_grouped(nc.vector.tensor_copy, w2_bank, w2_g.bitcast(F32))
        w2_c = const.tile([P, 2 * Z], U32, name="w2_c", align_bytes=64)
        w2_s = const.tile([P, 2 * Z], U8, name="w2_s", align_bytes=64)
        nc.vector.quantize_mx(out=w2_c.bitcast(FP8X4), scales=w2_s, in_=w2_g)

        for i in range(NCH + 3):
            if live(i - 1):
                for t in range(H_TILES):
                    relu_group(i - 1, t)
                    if t + LEAD < H_TILES:
                        hidden_group(i - 1, t + LEAD)
            if live(i - 2):
                add_bias_logvar(i - 2)
                add_bias_mean(i - 2)
                clip_logvar(i - 2)
                mean_difference(i - 2)
                logvar_difference(i - 2)
                scale_difference(i - 2)
            if live(i):
                for q in range(4):
                    empty_bank(4 * i + q)
                    if 4 * i + q + LEAD < 4 * NCH:
                        fill_bank(4 * i + q + LEAD)
            if live(i - 1):
                regroup_hidden(i - 1)
            if live(i - 3):
                scale_noise(i - 3)
            if live(i - 1):
                quantise_hidden(i - 1)
                stats_matmuls(i - 1)
            if live(i - 3):
                add_mean(i - 3)
            if live(i):
                quantise_inputs(i)
                for t in range(LEAD):
                    hidden_group(i, t)
            if live(i - 2):
                posterior_sd(i - 2)
            if live(i - 1):
                prior_inverse_sd(i - 1)
            if live(i - 2):
                row_sums(i - 2, ACT.Exp, dlv[i - 2], sum_ex, "ex_unread")
                row_sums(i - 2, ACT.Square, ratio[i - 2], sum_sq, "sq_unread")

        total = const.tile([P, TILES], F32, name="total")
        nc.vector.tensor_tensor(out=total, in0=sum_sq, in1=sum_ex, op=ALU.add)
        total2 = const.tile([P, TILES], F32, name="total2")
        nc.vector.tensor_tensor(out=total2, in0=total, in1=sum_df, op=ALU.subtract)
        kl = const.tile([P, TILES], F32, name="kl")
        nc.vector.tensor_scalar(out=kl, in0=total2, scalar1=0.5, scalar2=-0.5 * Z, op0=ALU.mult, op1=ALU.add)
        nc.sync.dma_start(out=kl_out.rearrange("(p j) -> p j", j=TILES), in_=kl)
